import numpy as np
import ml_dtypes


def mxq(x, axis, fmt="e4m3"):
    dtype, down = {"e4m3": (ml_dtypes.float8_e4m3fn, 7), "e5m2": (ml_dtypes.float8_e5m2, 14)}[fmt]
    v = np.moveaxis(np.asarray(x, np.float32).astype(ml_dtypes.bfloat16).astype(np.float64), axis, -1)
    blocks = v.reshape(v.shape[:-1] + (-1, 32))
    amax = np.abs(blocks).max(-1, keepdims=True)
    byte = np.maximum(np.where(amax > 0, np.frexp(amax)[1] - 1 + 127, 0) - down, 1)
    scale = np.exp2(byte - 127.0)
    codes = (blocks / scale).astype(np.float32).astype(dtype).astype(np.float64)
    return np.moveaxis((codes * scale).reshape(v.shape), -1, axis)


WIDE = False


def mx_kscale(k):
    if not WIDE:
        return np.ones(k)
    levels = np.array([10, -10, 5, -5, 0])
    if k % 512:
        return np.exp2(np.random.permutation(np.resize(levels, k // 32))).repeat(32)
    a = np.empty((k // 512, 16))
    for p in range(k // 512):
        a[p, :8] = np.random.permutation(np.resize(levels, 8))
        for g in range(8):
            far = levels[np.abs(levels - a[p, g]) >= 10]
            a[p, g + 8] = far[np.random.randint(len(far))]
    return np.exp2(a.ravel()).repeat(32)


BF16 = ml_dtypes.bfloat16


def bf(x):
    return np.asarray(x, np.float32).astype(BF16)


def f64(x):
    return np.asarray(x).astype(np.float64)


B, S, IN, OUT = 4, 32, 1024, 1024


def setup_inputs():
    s = mx_kscale(IN)
    w = np.random.standard_normal((OUT, IN + 1))
    w[:, :IN] *= 0.25 / np.sqrt(IN) / s
    w[:, IN] *= 0.5
    return {"x": bf(np.random.standard_normal((B, S, IN)) * s), "weight": bf(w)}


def reference(x, weight):
    w = f64(weight)
    in_features = w.shape[1] - 1
    xf = f64(x).reshape(-1, in_features)
    wm, wb = w[:, :in_features], w[:, in_features]
    xq = mxq(xf, 1, "e4m3")
    wq = mxq(wm, 1, "e4m3")
    lin = (xq @ wq.T) + wb
    ab = (np.abs(xq) @ np.abs(wq).T) + np.abs(wb)
    return 0.5 * (lin + ab)

@@ -1,0 +1,191 @@
+from contextlib import ExitStack
+
+import concourse.mybir as mybir
+from concourse.masks import make_identity
+
+F32 = mybir.dt.float32
+BF16 = mybir.dt.bfloat16
+I32 = mybir.dt.int32
+U32 = mybir.dt.uint32
+U8 = mybir.dt.uint8
+FP8X4 = mybir.dt.float8_e4m3fn_x4
+ALU = mybir.AluOpType
+ACT = mybir.ActivationFunctionType
+
+P = 128
+IN = 1024
+OUT = 1024
+BANK = 512
+PACK = 4
+PASSES = IN // (P * PACK)
+WORD_BLOCKS = IN // 2 // P
+SIGNS = 2
+TERMS = SIGNS * PASSES
+UNITS = 2
+CHUNK = UNITS * P
+CHUNKS = OUT // CHUNK
+W_PITCH = 1040
+CLEAR_SIGNS = 0x7FFF7FFF
+
+FLOPS = 2 * 2 * P * IN * OUT
+
+
+def tile_skanlinear_s_kernel(tc, x, weight, out):
+    nc = tc.nc
+
+    with ExitStack() as ctx:
+        const = ctx.enter_context(tc.tile_pool(name="const", bufs=1))
+        keep = ctx.enter_context(tc.tile_pool(name="keep", bufs=1))
+        flipped = ctx.enter_context(tc.psum_pool(name="flipped", bufs=2 * UNITS))
+        rows_out = ctx.enter_context(tc.psum_pool(name="rows_out", bufs=1))
+        ctx.enter_context(tc.manual_schedule())
+
+        def operand_tiles(name, n_rows):
+            n_words = TERMS * n_rows
+            return {
+                "grouped": keep.tile([P, n_words * PACK], BF16, name=name + "_grouped", align_bytes=64),
+                "codes": keep.tile([P, n_words], U32, name=name + "_codes", align_bytes=64),
+                "scales": keep.tile([P, n_words], U8, name=name + "_scales", align_bytes=64),
+            }
+
+        x_rows = keep.tile([P, 1, IN], BF16)
+        x_mx = operand_tiles("x", P)
+        w_rows = [keep.tile([P, UNITS, W_PITCH], BF16, name="w_rows%d" % c) for c in range(CHUNKS)]
+        w_mx = [operand_tiles("w%d" % c, CHUNK) for c in range(CHUNKS)]
+        bias = keep.tile([P, OUT], F32)
+        y = [keep.tile([P, CHUNK], F32, name="y%d" % c) for c in range(CHUNKS)]
+        bias_banks = [rows_out.tile([P, BANK], F32, name="bias_bank%d" % b) for b in range(OUT // BANK)]
+        sum_banks = [rows_out.tile([P, BANK], F32, name="sum_bank%d" % b) for b in range(OUT // BANK)]
+
+        def in_bank(banks, first, width):
+            return banks[first // BANK][:, first % BANK : first % BANK + width]
+
+        nc.sync.dma_start(out=x_rows[:, 0, :], in_=x.flatten_outer_dims())
+        for c in range(CHUNKS):
+            for j in range(UNITS):
+                first_row = c * CHUNK + j * P
+                nc.sync.dma_start(
+                    out=w_rows[c][:, j, 0 : IN + 1], in_=weight[first_row : first_row + P, :]
+                )
+
+        ident_f32 = const.tile([P, P], F32)
+        make_identity(nc, ident_f32[:])
+        ident_bf16 = const.tile([P, P], BF16)
+        make_identity(nc, ident_bf16[:])
+
+        warm = const.tile([P, 1], F32)
+        nc.vector.memset(warm[:], 0.0)
+        nc.scalar.activation(out=warm[:], in_=warm[:], func=ACT.Abs)
+
+        def flip(rows, mx):
+            words = mx["grouped"][:].bitcast(F32).rearrange(
+                "p (s g r u) -> p s g r u", s=SIGNS, g=PASSES, u=2
+            )
+            flip_banks = []
+            for j in range(rows.shape[1]):
+                row_words = rows[:, j, 0:IN].bitcast(F32)
+                flip_bank = flipped.tile([P, WORD_BLOCKS, P], F32, name="flip_bank")
+                for m in range(WORD_BLOCKS):
+                    g, u = divmod(m, 2)
+                    nc.tensor.transpose(
+                        flip_bank[:, m, :],
+                        row_words[:, 2 * P * g + u : 2 * P * (g + 1) : 2],
+                        ident_f32[:],
+                    )
+                nc.scalar.copy(
+                    out=words[:, 0, :, j * P : (j + 1) * P, :],
+                    in_=flip_bank[:].rearrange("p (g u) r -> p g r u", u=2),
+                )
+                flip_banks.append(flip_bank)
+            return flip_banks
+
+        def spread_wb(c):
+            for j in range(UNITS):
+                nc.tensor.matmul(
+                    out=in_bank(bias_banks, c * CHUNK + j * P, P),
+                    lhsT=w_rows[c][:, j, IN : IN + 1].to_broadcast([P, P]),
+                    rhs=ident_bf16[:],
+                    start=True,
+                    stop=True,
+                )
+
+        def scalar_absolute(flip_banks, mx):
+            values = mx["grouped"][:].rearrange(
+                "p (s g r u e) -> p s g r u e", s=SIGNS, g=PASSES, u=2, e=2
+            )
+            for j, flip_bank in enumerate(flip_banks):
+                pairs = flip_bank[:].bitcast(BF16).rearrange(
+                    "p (g u) (r e) -> p g r u e", u=2, e=2
+                )
+                for g in range(PASSES):
+                    nc.scalar.activation(
+                        out=values[:, 1, g, j * P : (j + 1) * P, :, :],
+                        in_=pairs[:, g, :, :, :],
+                        func=ACT.Abs,
+                    )
+
+        def clear_signs(mx):
+            ints = mx["grouped"][:].bitcast(I32)
+            half = ints.shape[1] // SIGNS
+            nc.vector.tensor_scalar(
+                out=ints[:, half:],
+                in0=ints[:, :half],
+                scalar1=CLEAR_SIGNS,
+                scalar2=None,
+                op0=ALU.bitwise_and,
+            )
+
+        def quantise(mx, s):
+            n_words = mx["codes"].shape[1] // SIGNS
+            word_cols = slice(s * n_words, (s + 1) * n_words)
+            nc.vector.quantize_mx(
+                out=mx["codes"][:, word_cols].bitcast(FP8X4),
+                scales=mx["scales"][:, word_cols],
+                in_=mx["grouped"][:, s * n_words * PACK : (s + 1) * n_words * PACK],
+            )
+
+        def multiply(c):
+            for i in range(TERMS):
+                nc.tensor.matmul_mx(
+                    out=in_bank(sum_banks, c * CHUNK, CHUNK),
+                    lhsT=x_mx["codes"][:, i * P : (i + 1) * P].bitcast(FP8X4),
+                    lhsT_scale=x_mx["scales"][:, i * P : (i + 1) * P],
+                    rhs=w_mx[c]["codes"][:, i * CHUNK : (i + 1) * CHUNK].bitcast(FP8X4),
+                    rhs_scale=w_mx[c]["scales"][:, i * CHUNK : (i + 1) * CHUNK],
+                    start=(i == 0),
+                    stop=(i == TERMS - 1),
+                )
+
+        def finish(c):
+            nc.vector.scalar_tensor_tensor(
+                out=y[c][:],
+                in0=in_bank(sum_banks, c * CHUNK, CHUNK),
+                scalar=0.5,
+                in1=bias[:, c * CHUNK : (c + 1) * CHUNK],
+                op0=ALU.mult,
+                op1=ALU.add,
+            )
+            nc.sync.dma_start(out=out[:, c * CHUNK : (c + 1) * CHUNK], in_=y[c][:])
+
+        last = CHUNKS - 1
+        flip(x_rows, x_mx)
+        w_flipped = [flip(w_rows[c], w_mx[c]) for c in range(CHUNKS)]
+        scalar_absolute(w_flipped[last], w_mx[last])
+        for c in range(CHUNKS):
+            spread_wb(c)
+        for b, bias_bank in enumerate(bias_banks):
+            nc.scalar.activation(
+                out=bias[:, b * BANK : (b + 1) * BANK], in_=bias_bank[:], func=ACT.Relu
+            )
+
+        clear_signs(x_mx)
+        quantise(x_mx, 0)
+        quantise(x_mx, 1)
+        for c in range(CHUNKS):
+            if c != last:
+                clear_signs(w_mx[c])
+            quantise(w_mx[c], 0)
+            quantise(w_mx[c], 1)
+            multiply(c)
+        for c in range(CHUNKS):
+            finish(c)

@@ -21,9 +21,11 @@ PASSES = IN // (P * PACK)
 WORD_BLOCKS = IN // 2 // P
 SIGNS = 2
 TERMS = SIGNS * PASSES
-UNITS = 2
-CHUNK = UNITS * P
-CHUNKS = OUT // CHUNK
+CHUNK_UNITS = (1, 1, 2, 2, 2)
+CHUNKS = len(CHUNK_UNITS)
+CHUNK_FIRST = [P * sum(CHUNK_UNITS[:c]) for c in range(CHUNKS)]
+CHUNK_ROWS = [P * n for n in CHUNK_UNITS]
+STORE = 256
 W_PITCH = 1040
 CLEAR_SIGNS = 0x7FFF7FFF
 
@@ -36,7 +38,7 @@ def tile_skanlinear_s_kernel(tc, x, weight, out):
     with ExitStack() as ctx:
         const = ctx.enter_context(tc.tile_pool(name="const", bufs=1))
         keep = ctx.enter_context(tc.tile_pool(name="keep", bufs=1))
-        flipped = ctx.enter_context(tc.psum_pool(name="flipped", bufs=2 * UNITS))
+        flipped = ctx.enter_context(tc.psum_pool(name="flipped", bufs=4))
         rows_out = ctx.enter_context(tc.psum_pool(name="rows_out", bufs=1))
         ctx.enter_context(tc.manual_schedule())
 
@@ -50,10 +52,12 @@ def tile_skanlinear_s_kernel(tc, x, weight, out):
 
         x_rows = keep.tile([P, 1, IN], BF16)
         x_mx = operand_tiles("x", P)
-        w_rows = [keep.tile([P, UNITS, W_PITCH], BF16, name="w_rows%d" % c) for c in range(CHUNKS)]
-        w_mx = [operand_tiles("w%d" % c, CHUNK) for c in range(CHUNKS)]
+        w_rows = [
+            keep.tile([P, n, W_PITCH], BF16, name="w_rows%d" % c) for c, n in enumerate(CHUNK_UNITS)
+        ]
+        w_mx = [operand_tiles("w%d" % c, n) for c, n in enumerate(CHUNK_ROWS)]
         bias = keep.tile([P, OUT], F32)
-        y = [keep.tile([P, CHUNK], F32, name="y%d" % c) for c in range(CHUNKS)]
+        y = [keep.tile([P, STORE], F32, name="y%d" % i) for i in range(OUT // STORE)]
         bias_banks = [rows_out.tile([P, BANK], F32, name="bias_bank%d" % b) for b in range(OUT // BANK)]
         sum_banks = [rows_out.tile([P, BANK], F32, name="sum_bank%d" % b) for b in range(OUT // BANK)]
 
@@ -62,8 +66,8 @@ def tile_skanlinear_s_kernel(tc, x, weight, out):
 
         nc.sync.dma_start(out=x_rows[:, 0, :], in_=x.flatten_outer_dims())
         for c in range(CHUNKS):
-            for j in range(UNITS):
-                first_row = c * CHUNK + j * P
+            for j in range(CHUNK_UNITS[c]):
+                first_row = CHUNK_FIRST[c] + j * P
                 nc.sync.dma_start(
                     out=w_rows[c][:, j, 0 : IN + 1], in_=weight[first_row : first_row + P, :]
                 )
@@ -76,6 +80,22 @@ def tile_skanlinear_s_kernel(tc, x, weight, out):
         warm = const.tile([P, 1], F32)
         nc.vector.memset(warm[:], 0.0)
         nc.scalar.activation(out=warm[:], in_=warm[:], func=ACT.Abs)
+
+        def flip_x():
+            words = x_mx["grouped"][:].bitcast(F32).rearrange(
+                "p (s g r u) -> p s g r u", s=SIGNS, g=PASSES, u=2
+            )
+            row_words = x_rows[:, 0, :].bitcast(F32)
+            for g in range(PASSES):
+                flip_bank = flipped.tile([P, WORD_BLOCKS, P], F32, name="flip_bank")
+                for u in range(2):
+                    nc.tensor.transpose(
+                        flip_bank[:, u, :],
+                        row_words[:, 2 * P * g + u : 2 * P * (g + 1) : 2],
+                        ident_f32[:],
+                    )
+                empty = nc.vector.tensor_copy if g == 0 else nc.scalar.copy
+                empty(out=words[:, 0, g, :, :], in_=flip_bank[:, 0:2, :].rearrange("p u r -> p r u"))
 
         def flip(rows, mx):
             words = mx["grouped"][:].bitcast(F32).rearrange(
@@ -100,9 +120,9 @@ def tile_skanlinear_s_kernel(tc, x, weight, out):
             return flip_banks
 
         def spread_wb(c):
-            for j in range(UNITS):
+            for j in range(CHUNK_UNITS[c]):
                 nc.tensor.matmul(
-                    out=in_bank(bias_banks, c * CHUNK + j * P, P),
+                    out=in_bank(bias_banks, CHUNK_FIRST[c] + j * P, P),
                     lhsT=w_rows[c][:, j, IN : IN + 1].to_broadcast([P, P]),
                     rhs=ident_bf16[:],
                     start=True,
@@ -145,30 +165,32 @@ def tile_skanlinear_s_kernel(tc, x, weight, out):
             )
 
         def multiply(c):
+            n = CHUNK_ROWS[c]
             for i in range(TERMS):
                 nc.tensor.matmul_mx(
-                    out=in_bank(sum_banks, c * CHUNK, CHUNK),
+                    out=in_bank(sum_banks, CHUNK_FIRST[c], n),
                     lhsT=x_mx["codes"][:, i * P : (i + 1) * P].bitcast(FP8X4),
                     lhsT_scale=x_mx["scales"][:, i * P : (i + 1) * P],
-                    rhs=w_mx[c]["codes"][:, i * CHUNK : (i + 1) * CHUNK].bitcast(FP8X4),
-                    rhs_scale=w_mx[c]["scales"][:, i * CHUNK : (i + 1) * CHUNK],
+                    rhs=w_mx[c]["codes"][:, i * n : (i + 1) * n].bitcast(FP8X4),
+                    rhs_scale=w_mx[c]["scales"][:, i * n : (i + 1) * n],
                     start=(i == 0),
                     stop=(i == TERMS - 1),
                 )
 
-        def finish(c):
+        def finish(i):
+            cols = slice(i * STORE, (i + 1) * STORE)
             nc.vector.scalar_tensor_tensor(
-                out=y[c][:],
-                in0=in_bank(sum_banks, c * CHUNK, CHUNK),
+                out=y[i][:],
+                in0=in_bank(sum_banks, i * STORE, STORE),
                 scalar=0.5,
-                in1=bias[:, c * CHUNK : (c + 1) * CHUNK],
+                in1=bias[:, cols],
                 op0=ALU.mult,
                 op1=ALU.add,
             )
-            nc.sync.dma_start(out=out[:, c * CHUNK : (c + 1) * CHUNK], in_=y[c][:])
+            nc.sync.dma_start(out=out[:, cols], in_=y[i][:])
 
         last = CHUNKS - 1
-        flip(x_rows, x_mx)
+        flip_x()
         w_flipped = [flip(w_rows[c], w_mx[c]) for c in range(CHUNKS)]
         scalar_absolute(w_flipped[last], w_mx[last])
         for c in range(CHUNKS):
@@ -187,5 +209,5 @@ def tile_skanlinear_s_kernel(tc, x, weight, out):
             quantise(w_mx[c], 0)
             quantise(w_mx[c], 1)
             multiply(c)
-        for c in range(CHUNKS):
-            finish(c)
+        for i in range(OUT // STORE):
+            finish(i)

@@ -56,9 +56,10 @@ def tile_skanlinear_s_kernel(tc, x, weight, out):
             keep.tile([P, n, W_PITCH], BF16, name="w_rows%d" % c) for c, n in enumerate(CHUNK_UNITS)
         ]
         w_mx = [operand_tiles("w%d" % c, n) for c, n in enumerate(CHUNK_ROWS)]
-        bias = keep.tile([P, OUT], F32)
+        bias_cols = keep.tile([P, OUT // P], BF16)
+        bias = keep.tile([P, OUT], BF16)
         y = [keep.tile([P, STORE], F32, name="y%d" % i) for i in range(OUT // STORE)]
-        bias_banks = [rows_out.tile([P, BANK], F32, name="bias_bank%d" % b) for b in range(OUT // BANK)]
+        bias_bank = rows_out.tile([P, OUT], BF16)
         sum_banks = [rows_out.tile([P, BANK], F32, name="sum_bank%d" % b) for b in range(OUT // BANK)]
 
         def in_bank(banks, first, width):
@@ -119,15 +120,23 @@ def tile_skanlinear_s_kernel(tc, x, weight, out):
                 flip_banks.append(flip_bank)
             return flip_banks
 
-        def spread_wb(c):
-            for j in range(CHUNK_UNITS[c]):
+        def relu_wb():
+            for c, n in enumerate(CHUNK_UNITS):
+                first = CHUNK_FIRST[c] // P
+                nc.scalar.activation(
+                    out=bias_cols[:, first : first + n], in_=w_rows[c][:, :, IN], func=ACT.Relu
+                )
+
+        def spread_wb():
+            for u in range(OUT // P):
                 nc.tensor.matmul(
-                    out=in_bank(bias_banks, CHUNK_FIRST[c] + j * P, P),
-                    lhsT=w_rows[c][:, j, IN : IN + 1].to_broadcast([P, P]),
+                    out=bias_bank[:, u * P : (u + 1) * P],
+                    lhsT=bias_cols[:, u : u + 1].to_broadcast([P, P]),
                     rhs=ident_bf16[:],
                     start=True,
                     stop=True,
                 )
+            nc.scalar.copy(out=bias[:], in_=bias_bank[:])
 
         def scalar_absolute(flip_banks, mx):
             values = mx["grouped"][:].rearrange(
@@ -192,13 +201,9 @@ def tile_skanlinear_s_kernel(tc, x, weight, out):
         last = CHUNKS - 1
         flip_x()
         w_flipped = [flip(w_rows[c], w_mx[c]) for c in range(CHUNKS)]
+        relu_wb()
+        spread_wb()
         scalar_absolute(w_flipped[last], w_mx[last])
-        for c in range(CHUNKS):
-            spread_wb(c)
-        for b, bias_bank in enumerate(bias_banks):
-            nc.scalar.activation(
-                out=bias[:, b * BANK : (b + 1) * BANK], in_=bias_bank[:], func=ACT.Relu
-            )
 
         clear_signs(x_mx)
         quantise(x_mx, 0)
@@ -207,7 +212,10 @@ def tile_skanlinear_s_kernel(tc, x, weight, out):
             if c != last:
                 clear_signs(w_mx[c])
             quantise(w_mx[c], 0)
+            if c == last:
+                finish(0)
+                finish(1)
             quantise(w_mx[c], 1)
             multiply(c)
-        for i in range(OUT // STORE):
-            finish(i)
+        finish(2)
+        finish(3)

@@ -120,12 +120,13 @@ def tile_skanlinear_s_kernel(tc, x, weight, out):
                 flip_banks.append(flip_bank)
             return flip_banks
 
-        def relu_wb():
-            for c, n in enumerate(CHUNK_UNITS):
-                first = CHUNK_FIRST[c] // P
-                nc.scalar.activation(
-                    out=bias_cols[:, first : first + n], in_=w_rows[c][:, :, IN], func=ACT.Relu
-                )
+        def relu_wb(c):
+            first = CHUNK_FIRST[c] // P
+            nc.scalar.activation(
+                out=bias_cols[:, first : first + CHUNK_UNITS[c]],
+                in_=w_rows[c][:, :, IN],
+                func=ACT.Relu,
+            )
 
         def spread_wb():
             for u in range(OUT // P):
@@ -136,7 +137,6 @@ def tile_skanlinear_s_kernel(tc, x, weight, out):
                     start=True,
                     stop=True,
                 )
-            nc.scalar.copy(out=bias[:], in_=bias_bank[:])
 
         def scalar_absolute(flip_banks, mx):
             values = mx["grouped"][:].rearrange(
@@ -200,10 +200,13 @@ def tile_skanlinear_s_kernel(tc, x, weight, out):
 
         last = CHUNKS - 1
         flip_x()
-        w_flipped = [flip(w_rows[c], w_mx[c]) for c in range(CHUNKS)]
-        relu_wb()
+        w_flipped = []
+        for c in range(CHUNKS):
+            relu_wb(c)
+            w_flipped.append(flip(w_rows[c], w_mx[c]))
         spread_wb()
         scalar_absolute(w_flipped[last], w_mx[last])
+        nc.scalar.copy(out=bias[:], in_=bias_bank[:])
 
         clear_signs(x_mx)
         quantise(x_mx, 0)
@@ -212,10 +215,7 @@ def tile_skanlinear_s_kernel(tc, x, weight, out):
             if c != last:
                 clear_signs(w_mx[c])
             quantise(w_mx[c], 0)
-            if c == last:
-                finish(0)
-                finish(1)
             quantise(w_mx[c], 1)
             multiply(c)
-        finish(2)
-        finish(3)
+        for i in range(OUT // STORE):
+            finish(i)

@@ -21,7 +21,7 @@ PASSES = IN // (P * PACK)
 WORD_BLOCKS = IN // 2 // P
 SIGNS = 2
 TERMS = SIGNS * PASSES
-CHUNK_UNITS = (1, 1, 2, 2, 2)
+CHUNK_UNITS = (1, 1, 2, 2, 1, 1)
 CHUNKS = len(CHUNK_UNITS)
 CHUNK_FIRST = [P * sum(CHUNK_UNITS[:c]) for c in range(CHUNKS)]
 CHUNK_ROWS = [P * n for n in CHUNK_UNITS]

from contextlib import ExitStack

import concourse.mybir as mybir
from concourse.masks import make_identity

F32 = mybir.dt.float32
BF16 = mybir.dt.bfloat16
I32 = mybir.dt.int32
U32 = mybir.dt.uint32
U8 = mybir.dt.uint8
FP8X4 = mybir.dt.float8_e4m3fn_x4
ALU = mybir.AluOpType
ACT = mybir.ActivationFunctionType

P = 128
IN = 1024
OUT = 1024
BANK = 512
PACK = 4
PASSES = IN // (P * PACK)
WORD_BLOCKS = IN // 2 // P
SIGNS = 2
TERMS = SIGNS * PASSES
CHUNK_UNITS = (1, 1, 2, 2, 1, 1)
CHUNKS = len(CHUNK_UNITS)
CHUNK_FIRST = [P * sum(CHUNK_UNITS[:c]) for c in range(CHUNKS)]
CHUNK_ROWS = [P * n for n in CHUNK_UNITS]
STORE = 256
W_PITCH = 1040
CLEAR_SIGNS = 0x7FFF7FFF

FLOPS = 2 * 2 * P * IN * OUT


def tile_skanlinear_s_kernel(tc, x, weight, out):
    nc = tc.nc

    with ExitStack() as ctx:
        const = ctx.enter_context(tc.tile_pool(name="const", bufs=1))
        keep = ctx.enter_context(tc.tile_pool(name="keep", bufs=1))
        flipped = ctx.enter_context(tc.psum_pool(name="flipped", bufs=4))
        rows_out = ctx.enter_context(tc.psum_pool(name="rows_out", bufs=1))
        ctx.enter_context(tc.manual_schedule())

        def operand_tiles(name, n_rows):
            n_words = TERMS * n_rows
            return {
                "grouped": keep.tile([P, n_words * PACK], BF16, name=name + "_grouped", align_bytes=64),
                "codes": keep.tile([P, n_words], U32, name=name + "_codes", align_bytes=64),
                "scales": keep.tile([P, n_words], U8, name=name + "_scales", align_bytes=64),
            }

        x_rows = keep.tile([P, 1, IN], BF16)
        x_mx = operand_tiles("x", P)
        w_rows = [
            keep.tile([P, n, W_PITCH], BF16, name="w_rows%d" % c) for c, n in enumerate(CHUNK_UNITS)
        ]
        w_mx = [operand_tiles("w%d" % c, n) for c, n in enumerate(CHUNK_ROWS)]
        bias_cols = keep.tile([P, OUT // P], BF16)
        bias = keep.tile([P, OUT], BF16)
        y = [keep.tile([P, STORE], F32, name="y%d" % i) for i in range(OUT // STORE)]
        bias_bank = rows_out.tile([P, OUT], BF16)
        sum_banks = [rows_out.tile([P, BANK], F32, name="sum_bank%d" % b) for b in range(OUT // BANK)]

        def in_bank(banks, first, width):
            return banks[first // BANK][:, first % BANK : first % BANK + width]

        nc.sync.dma_start(out=x_rows[:, 0, :], in_=x.flatten_outer_dims())
        for c in range(CHUNKS):
            for j in range(CHUNK_UNITS[c]):
                first_row = CHUNK_FIRST[c] + j * P
                nc.sync.dma_start(
                    out=w_rows[c][:, j, 0 : IN + 1], in_=weight[first_row : first_row + P, :]
                )

        ident_f32 = const.tile([P, P], F32)
        make_identity(nc, ident_f32[:])
        ident_bf16 = const.tile([P, P], BF16)
        make_identity(nc, ident_bf16[:])

        warm = const.tile([P, 1], F32)
        nc.vector.memset(warm[:], 0.0)
        nc.scalar.activation(out=warm[:], in_=warm[:], func=ACT.Abs)

        def flip_x():
            words = x_mx["grouped"][:].bitcast(F32).rearrange(
                "p (s g r u) -> p s g r u", s=SIGNS, g=PASSES, u=2
            )
            row_words = x_rows[:, 0, :].bitcast(F32)
            for g in range(PASSES):
                flip_bank = flipped.tile([P, WORD_BLOCKS, P], F32, name="flip_bank")
                for u in range(2):
                    nc.tensor.transpose(
                        flip_bank[:, u, :],
                        row_words[:, 2 * P * g + u : 2 * P * (g + 1) : 2],
                        ident_f32[:],
                    )
                empty = nc.vector.tensor_copy if g == 0 else nc.scalar.copy
                empty(out=words[:, 0, g, :, :], in_=flip_bank[:, 0:2, :].rearrange("p u r -> p r u"))

        def flip(rows, mx):
            words = mx["grouped"][:].bitcast(F32).rearrange(
                "p (s g r u) -> p s g r u", s=SIGNS, g=PASSES, u=2
            )
            flip_banks = []
            for j in range(rows.shape[1]):
                row_words = rows[:, j, 0:IN].bitcast(F32)
                flip_bank = flipped.tile([P, WORD_BLOCKS, P], F32, name="flip_bank")
                for m in range(WORD_BLOCKS):
                    g, u = divmod(m, 2)
                    nc.tensor.transpose(
                        flip_bank[:, m, :],
                        row_words[:, 2 * P * g + u : 2 * P * (g + 1) : 2],
                        ident_f32[:],
                    )
                nc.scalar.copy(
                    out=words[:, 0, :, j * P : (j + 1) * P, :],
                    in_=flip_bank[:].rearrange("p (g u) r -> p g r u", u=2),
                )
                flip_banks.append(flip_bank)
            return flip_banks

        def relu_wb(c):
            first = CHUNK_FIRST[c] // P
            nc.scalar.activation(
                out=bias_cols[:, first : first + CHUNK_UNITS[c]],
                in_=w_rows[c][:, :, IN],
                func=ACT.Relu,
            )

        def spread_wb():
            for u in range(OUT // P):
                nc.tensor.matmul(
                    out=bias_bank[:, u * P : (u + 1) * P],
                    lhsT=bias_cols[:, u : u + 1].to_broadcast([P, P]),
                    rhs=ident_bf16[:],
                    start=True,
                    stop=True,
                )

        def scalar_absolute(flip_banks, mx):
            values = mx["grouped"][:].rearrange(
                "p (s g r u e) -> p s g r u e", s=SIGNS, g=PASSES, u=2, e=2
            )
            for j, flip_bank in enumerate(flip_banks):
                pairs = flip_bank[:].bitcast(BF16).rearrange(
                    "p (g u) (r e) -> p g r u e", u=2, e=2
                )
                for g in range(PASSES):
                    nc.scalar.activation(
                        out=values[:, 1, g, j * P : (j + 1) * P, :, :],
                        in_=pairs[:, g, :, :, :],
                        func=ACT.Abs,
                    )

        def clear_signs(mx):
            ints = mx["grouped"][:].bitcast(I32)
            half = ints.shape[1] // SIGNS
            nc.vector.tensor_scalar(
                out=ints[:, half:],
                in0=ints[:, :half],
                scalar1=CLEAR_SIGNS,
                scalar2=None,
                op0=ALU.bitwise_and,
            )

        def quantise(mx, s):
            n_words = mx["codes"].shape[1] // SIGNS
            word_cols = slice(s * n_words, (s + 1) * n_words)
            nc.vector.quantize_mx(
                out=mx["codes"][:, word_cols].bitcast(FP8X4),
                scales=mx["scales"][:, word_cols],
                in_=mx["grouped"][:, s * n_words * PACK : (s + 1) * n_words * PACK],
            )

        def multiply(c):
            n = CHUNK_ROWS[c]
            for i in range(TERMS):
                nc.tensor.matmul_mx(
                    out=in_bank(sum_banks, CHUNK_FIRST[c], n),
                    lhsT=x_mx["codes"][:, i * P : (i + 1) * P].bitcast(FP8X4),
                    lhsT_scale=x_mx["scales"][:, i * P : (i + 1) * P],
                    rhs=w_mx[c]["codes"][:, i * n : (i + 1) * n].bitcast(FP8X4),
                    rhs_scale=w_mx[c]["scales"][:, i * n : (i + 1) * n],
                    start=(i == 0),
                    stop=(i == TERMS - 1),
                )

        def finish(i):
            cols = slice(i * STORE, (i + 1) * STORE)
            nc.vector.scalar_tensor_tensor(
                out=y[i][:],
                in0=in_bank(sum_banks, i * STORE, STORE),
                scalar=0.5,
                in1=bias[:, cols],
                op0=ALU.mult,
                op1=ALU.add,
            )
            nc.sync.dma_start(out=out[:, cols], in_=y[i][:])

        last = CHUNKS - 1
        flip_x()
        w_flipped = []
        for c in range(CHUNKS):
            relu_wb(c)
            w_flipped.append(flip(w_rows[c], w_mx[c]))
        spread_wb()
        scalar_absolute(w_flipped[last], w_mx[last])
        nc.scalar.copy(out=bias[:], in_=bias_bank[:])

        clear_signs(x_mx)
        quantise(x_mx, 0)
        quantise(x_mx, 1)
        for c in range(CHUNKS):
            if c != last:
                clear_signs(w_mx[c])
            quantise(w_mx[c], 0)
            quantise(w_mx[c], 1)
            multiply(c)
        for i in range(OUT // STORE):
            finish(i)
